import numpy as np
import ml_dtypes


def mxq(x, axis, fmt="e4m3"):
    dtype, down = {"e4m3": (ml_dtypes.float8_e4m3fn, 7), "e5m2": (ml_dtypes.float8_e5m2, 14)}[fmt]
    v = np.moveaxis(np.asarray(x, np.float32).astype(ml_dtypes.bfloat16).astype(np.float64), axis, -1)
    blocks = v.reshape(v.shape[:-1] + (-1, 32))
    amax = np.abs(blocks).max(-1, keepdims=True)
    byte = np.maximum(np.where(amax > 0, np.frexp(amax)[1] - 1 + 127, 0) - down, 1)
    scale = np.exp2(byte - 127.0)
    codes = (blocks / scale).astype(np.float32).astype(dtype).astype(np.float64)
    return np.moveaxis((codes * scale).reshape(v.shape), -1, axis)


WIDE = False


def mx_kscale(k):
    if not WIDE:
        return np.ones(k)
    levels = np.array([10, -10, 5, -5, 0])
    if k % 512:
        return np.exp2(np.random.permutation(np.resize(levels, k // 32))).repeat(32)
    a = np.empty((k // 512, 16))
    for p in range(k // 512):
        a[p, :8] = np.random.permutation(np.resize(levels, 8))
        for g in range(8):
            far = levels[np.abs(levels - a[p, g]) >= 10]
            a[p, g + 8] = far[np.random.randint(len(far))]
    return np.exp2(a.ravel()).repeat(32)


BF16 = ml_dtypes.bfloat16


def bf(x):
    return np.asarray(x, np.float32).astype(BF16)


def f64(x):
    return np.asarray(x).astype(np.float64)


B, L, D, H = 1, 1024, 512, 8


def setup_inputs():
    s = mx_kscale(D)
    return {"x": bf(np.random.standard_normal((B, L, D)) * s),
            "w": bf(np.random.standard_normal((H, D, D)) / np.sqrt(D) / s[:, None] * s[None, :])}


def reference(x, w):
    wq = mxq(f64(w), 1, "e4m3")
    xq = mxq(f64(x), 2, "e4m3")
    xs = (xq[None] @ wq[:, None]).reshape(H * B, L, D)
    return mxq(xs, 2, "e4m3") @ wq

@@ -1,0 +1,200 @@
+from contextlib import ExitStack
+
+import concourse.mybir as mybir
+from concourse.masks import make_identity
+
+BF16 = mybir.dt.bfloat16
+F32 = mybir.dt.float32
+U32 = mybir.dt.uint32
+U8 = mybir.dt.uint8
+FP8X4 = mybir.dt.float8_e4m3fn_x4
+
+P = 128
+PACK = 4
+HEADS = 8
+TOKENS = 1024
+FEATURES = P * PACK
+TOKEN_TILES = TOKENS // P
+CHUNK = 4
+CHUNKS_PER_HEAD = TOKEN_TILES // CHUNK
+CHUNKS = HEADS * CHUNKS_PER_HEAD
+CHUNK_TOKENS = CHUNK * P
+SCALAR_XS_BANKS = 1
+SCALAR_XS_BANKS_FIRST_ROUND = 3
+SCALAR_XS_BANKS_LAST_ROUND = 0
+W_HALF = FEATURES // 2
+W_HALVES = 2 * HEADS
+
+FLOPS = 2 * 2 * HEADS * TOKENS * FEATURES * FEATURES
+
+
+def tile_multiheadattention_pa_kernel(tc, x, w, out):
+    nc = tc.nc
+    x_tiles = x[0].rearrange("(c r) k -> c r k", r=TOKEN_TILES)
+
+    with ExitStack() as ctx:
+        keep = ctx.enter_context(tc.tile_pool(name="keep", bufs=1))
+        stage = ctx.enter_context(tc.tile_pool(name="stage", bufs=2))
+        store = ctx.enter_context(tc.tile_pool(name="store", bufs=12))
+        psum = ctx.enter_context(tc.psum_pool(name="psum", bufs=CHUNK))
+        ctx.enter_context(tc.manual_schedule())
+
+        x_rows = keep.tile([P, TOKEN_TILES, FEATURES], BF16)
+        w_rows = [keep.tile([P, PACK, FEATURES], BF16, name="w_rows%d" % h) for h in range(HEADS)]
+
+        def load_x(half):
+            tiles = slice(half * CHUNK, (half + 1) * CHUNK)
+            nc.sync.dma_start(out=x_rows[:, tiles, :], in_=x_tiles[:, tiles, :])
+
+        def load_w(h):
+            nc.sync.dma_start(out=w_rows[h][:], in_=w[h].rearrange("(p t) n -> p t n", t=PACK))
+
+        load_x(0)
+        load_w(0)
+        load_x(1)
+        for h in range(1, HEADS):
+            load_w(h)
+
+        identity = keep.tile([P, P], F32)
+        make_identity(nc, identity[:])
+
+        w_codes = [keep.tile([P, FEATURES], U32, name="w_codes%d" % h, align_bytes=64) for h in range(HEADS)]
+        w_scales = [keep.tile([P, FEATURES], U8, name="w_scales%d" % h, align_bytes=64) for h in range(HEADS)]
+        w_grouped = [keep.tile([P, W_HALF, PACK], BF16, name="w_grouped%d" % s, align_bytes=64) for s in range(2)]
+
+        def regroup_w(m, on_gpsimd):
+            rows = w_rows[m // 2][:].rearrange("p t (c s) -> p s c t", s=PACK)
+            rows = rows[:, (m % 2) * 2 : (m % 2) * 2 + 2, :, :]
+            grouped = w_grouped[m % 2][:].rearrange("p (s c) t -> p s c t", s=2)
+            if on_gpsimd:
+                nc.gpsimd.tensor_scalar(
+                    out=grouped,
+                    in0=rows,
+                    scalar1=1.0,
+                    scalar2=0.0,
+                    op0=mybir.AluOpType.mult,
+                    op1=mybir.AluOpType.add,
+                )
+            else:
+                nc.vector.tensor_copy(out=grouped, in_=rows)
+
+        def quantise_w(m):
+            columns = slice((m % 2) * W_HALF, (m % 2 + 1) * W_HALF)
+            nc.vector.quantize_mx(
+                out=w_codes[m // 2][:, columns].bitcast(FP8X4),
+                scales=w_scales[m // 2][:, columns],
+                in_=w_grouped[m % 2][:].rearrange("p n t -> p (n t)"),
+            )
+
+        x_grouped = keep.tile([P, TOKEN_TILES, P * PACK], BF16, align_bytes=64)
+        x_codes = keep.tile([P, TOKENS], U32, align_bytes=64)
+        x_scales = keep.tile([P, TOKENS], U8, align_bytes=64)
+
+        def transpose_x(r):
+            x_bank = psum.tile([P, 2, P], F32, tag="xs_bank" if r < CHUNK else "out_bank")
+            words = x_rows[:, r, :].bitcast(F32)
+            for u in range(2):
+                nc.tensor.transpose(x_bank[:, u, :], words[:, u : 2 * P : 2], identity[:])
+            grouped_words = x_grouped[:, r, :].bitcast(F32)
+            nc.scalar.copy(
+                out=grouped_words.rearrange("p (c u) -> p c u", u=2),
+                in_=x_bank[:].rearrange("p u c -> p c u"),
+            )
+
+        def quantise_x(half):
+            tiles = slice(half * CHUNK, (half + 1) * CHUNK)
+            tokens = slice(half * CHUNK_TOKENS, (half + 1) * CHUNK_TOKENS)
+            nc.vector.quantize_mx(
+                out=x_codes[:, tokens].bitcast(FP8X4),
+                scales=x_scales[:, tokens],
+                in_=x_grouped[:, tiles, :].rearrange("p r k -> p (r k)"),
+            )
+
+        def first_matmul(j, i):
+            h = j // CHUNKS_PER_HEAD
+            r = (j % CHUNKS_PER_HEAD) * CHUNK + i
+            tokens = slice(r * P, (r + 1) * P)
+            xs_bank = psum.tile([P, PACK, P], F32, tag="xs_bank")
+            for t in range(PACK):
+                features = slice(t * P, (t + 1) * P)
+                nc.tensor.matmul_mx(
+                    out=xs_bank[:, t, :],
+                    lhsT=w_codes[h][:, features].bitcast(FP8X4),
+                    lhsT_scale=w_scales[h][:, features],
+                    rhs=x_codes[:, tokens].bitcast(FP8X4),
+                    rhs_scale=x_scales[:, tokens],
+                    start=True,
+                    stop=True,
+                )
+            return xs_bank
+
+        def second_matmul(j, i, xs_codes, xs_scales):
+            h = j // CHUNKS_PER_HEAD
+            tokens = slice(i * P, (i + 1) * P)
+            out_bank = psum.tile([P, FEATURES], F32, tag="out_bank")
+            nc.tensor.matmul_mx(
+                out=out_bank[:],
+                lhsT=xs_codes[:, tokens].bitcast(FP8X4),
+                lhsT_scale=xs_scales[:, tokens],
+                rhs=w_codes[h][:].bitcast(FP8X4),
+                rhs_scale=w_scales[h][:],
+                start=True,
+                stop=True,
+            )
+            return out_bank
+
+        def store_chunk(j, out_banks, copies):
+            h = j // CHUNKS_PER_HEAD
+            out_tiles = out[h].rearrange("(c r) e -> c r e", r=TOKEN_TILES)
+            for i in range(CHUNK):
+                out_rows = store.tile([P, FEATURES], F32)
+                copies[i % len(copies)](
+                    out=out_rows[:].rearrange("p (m t) -> p m t", t=PACK),
+                    in_=out_banks[i][:].rearrange("p (t m) -> p m t", t=PACK),
+                )
+                nc.sync.dma_start(out=out_tiles[:, (j % CHUNKS_PER_HEAD) * CHUNK + i, :], in_=out_rows[:])
+
+        for r in range(TOKEN_TILES):
+            transpose_x(r)
+        regroup_w(0, on_gpsimd=False)
+        regroup_w(1, on_gpsimd=False)
+        quantise_w(0)
+        quantise_w(1)
+        quantise_x(0)
+        regroup_w(2, on_gpsimd=False)
+        regroup_w(3, on_gpsimd=False)
+        quantise_w(2)
+        quantise_x(1)
+        regroup_w(4, on_gpsimd=False)
+        xs_banks = [first_matmul(0, i) for i in range(CHUNK)]
+        out_banks = []
+
+        for j in range(CHUNKS):
+            xs_grouped = stage.tile([P, CHUNK, P, PACK], BF16, align_bytes=64)
+            xs_codes = stage.tile([P, CHUNK_TOKENS], U32, align_bytes=64)
+            xs_scales = stage.tile([P, CHUNK_TOKENS], U8, align_bytes=64)
+            next_xs_banks = []
+            scalar_xs_banks = SCALAR_XS_BANKS
+            if j == 0:
+                scalar_xs_banks = SCALAR_XS_BANKS_FIRST_ROUND
+            if j == CHUNKS - 1:
+                scalar_xs_banks = SCALAR_XS_BANKS_LAST_ROUND
+            for i in range(CHUNK):
+                if i == scalar_xs_banks and j > 0:
+                    store_chunk(j - 1, out_banks, [nc.scalar.copy])
+                copy = nc.scalar.copy if i < scalar_xs_banks else nc.vector.tensor_copy
+                copy(out=xs_grouped[:, i, :, :], in_=xs_banks[i][:].rearrange("p t c -> p c t"))
+                if j + 1 < CHUNKS:
+                    next_xs_banks.append(first_matmul(j + 1, i))
+            if j + 3 < W_HALVES:
+                quantise_w(j + 3)
+            if j + 5 < W_HALVES:
+                regroup_w(j + 5, on_gpsimd=True)
+            nc.vector.quantize_mx(
+                out=xs_codes[:].bitcast(FP8X4),
+                scales=xs_scales[:],
+                in_=xs_grouped[:].rearrange("p i c t -> p (i c t)"),
+            )
+            out_banks = [second_matmul(j, i, xs_codes, xs_scales) for i in range(CHUNK)]
+            xs_banks = next_xs_banks
+        store_chunk(CHUNKS - 1, out_banks, [nc.scalar.copy, nc.vector.tensor_copy])

@@ -63,9 +63,9 @@ def tile_multiheadattention_pa_kernel(tc, x, w, out):
         w_grouped = [keep.tile([P, W_HALF, PACK], BF16, name="w_grouped%d" % s, align_bytes=64) for s in range(2)]
 
         def regroup_w(m, on_gpsimd):
-            rows = w_rows[m // 2][:].rearrange("p t (c s) -> p s c t", s=PACK)
-            rows = rows[:, (m % 2) * 2 : (m % 2) * 2 + 2, :, :]
-            grouped = w_grouped[m % 2][:].rearrange("p (s c) t -> p s c t", s=2)
+            rows = w_rows[m // 2][:].rearrange("p t (c s) -> p c s t", s=PACK)
+            rows = rows[:, :, (m % 2) * 2 : (m % 2) * 2 + 2, :]
+            grouped = w_grouped[m % 2][:].rearrange("p (s c) t -> p c s t", s=2)
             if on_gpsimd:
                 nc.gpsimd.tensor_scalar(
                     out=grouped,

@@ -19,11 +19,10 @@ CHUNK = 4
 CHUNKS_PER_HEAD = TOKEN_TILES // CHUNK
 CHUNKS = HEADS * CHUNKS_PER_HEAD
 CHUNK_TOKENS = CHUNK * P
-SCALAR_XS_BANKS = 1
-SCALAR_XS_BANKS_FIRST_ROUND = 3
-SCALAR_XS_BANKS_LAST_ROUND = 0
 W_HALF = FEATURES // 2
 W_HALVES = 2 * HEADS
+
+WARM_UP_MATMULS = 5
 
 FLOPS = 2 * 2 * HEADS * TOKENS * FEATURES * FEATURES
 
@@ -42,31 +41,39 @@ def tile_multiheadattention_pa_kernel(tc, x, w, out):
         x_rows = keep.tile([P, TOKEN_TILES, FEATURES], BF16)
         w_rows = [keep.tile([P, PACK, FEATURES], BF16, name="w_rows%d" % h) for h in range(HEADS)]
 
-        def load_x(half):
-            tiles = slice(half * CHUNK, (half + 1) * CHUNK)
+        def load_x(first, count):
+            tiles = slice(first, first + count)
             nc.sync.dma_start(out=x_rows[:, tiles, :], in_=x_tiles[:, tiles, :])
 
         def load_w(h):
             nc.sync.dma_start(out=w_rows[h][:], in_=w[h].rearrange("(p t) n -> p t n", t=PACK))
 
-        load_x(0)
         load_w(0)
-        load_x(1)
-        for h in range(1, HEADS):
+        load_x(0, 2)
+        load_x(2, 2)
+        load_w(1)
+        load_x(4, 4)
+        for h in range(2, HEADS):
             load_w(h)
 
         identity = keep.tile([P, P], F32)
         make_identity(nc, identity[:])
 
+        zeros = keep.tile([P, FEATURES], BF16)
+        nc.vector.memset(zeros[:], 0.0)
+        warm_bank = psum.tile([P, FEATURES], F32, tag="out_bank")
+        for n in range(WARM_UP_MATMULS):
+            nc.tensor.matmul(warm_bank[:], lhsT=zeros[:, :P], rhs=zeros[:], start=True, stop=True)
+
         w_codes = [keep.tile([P, FEATURES], U32, name="w_codes%d" % h, align_bytes=64) for h in range(HEADS)]
         w_scales = [keep.tile([P, FEATURES], U8, name="w_scales%d" % h, align_bytes=64) for h in range(HEADS)]
         w_grouped = [keep.tile([P, W_HALF, PACK], BF16, name="w_grouped%d" % s, align_bytes=64) for s in range(2)]
 
-        def regroup_w(m, on_gpsimd):
+        def regroup_w(m, engine):
             rows = w_rows[m // 2][:].rearrange("p t (c s) -> p c s t", s=PACK)
             rows = rows[:, :, (m % 2) * 2 : (m % 2) * 2 + 2, :]
-            grouped = w_grouped[m % 2][:].rearrange("p (s c) t -> p c s t", s=2)
-            if on_gpsimd:
+            grouped = w_grouped[0 if m in (0, 2) else 1][:].rearrange("p (s c) t -> p c s t", s=2)
+            if engine is nc.gpsimd:
                 nc.gpsimd.tensor_scalar(
                     out=grouped,
                     in0=rows,
@@ -75,6 +82,8 @@ def tile_multiheadattention_pa_kernel(tc, x, w, out):
                     op0=mybir.AluOpType.mult,
                     op1=mybir.AluOpType.add,
                 )
+            elif engine is nc.scalar:
+                nc.scalar.copy(out=grouped, in_=rows)
             else:
                 nc.vector.tensor_copy(out=grouped, in_=rows)
 
@@ -83,7 +92,7 @@ def tile_multiheadattention_pa_kernel(tc, x, w, out):
             nc.vector.quantize_mx(
                 out=w_codes[m // 2][:, columns].bitcast(FP8X4),
                 scales=w_scales[m // 2][:, columns],
-                in_=w_grouped[m % 2][:].rearrange("p n t -> p (n t)"),
+                in_=w_grouped[0 if m in (0, 2) else 1][:].rearrange("p n t -> p (n t)"),
             )
 
         x_grouped = keep.tile([P, TOKEN_TILES, P * PACK], BF16, align_bytes=64)
@@ -101,9 +110,9 @@ def tile_multiheadattention_pa_kernel(tc, x, w, out):
                 in_=x_bank[:].rearrange("p u c -> p c u"),
             )
 
-        def quantise_x(half):
-            tiles = slice(half * CHUNK, (half + 1) * CHUNK)
-            tokens = slice(half * CHUNK_TOKENS, (half + 1) * CHUNK_TOKENS)
+        def quantise_x(pair):
+            tiles = slice(pair * 2, (pair + 1) * 2)
+            tokens = slice(pair * 2 * P, (pair + 1) * 2 * P)
             nc.vector.quantize_mx(
                 out=x_codes[:, tokens].bitcast(FP8X4),
                 scales=x_scales[:, tokens],
@@ -126,75 +135,131 @@ def tile_multiheadattention_pa_kernel(tc, x, w, out):
                     start=True,
                     stop=True,
                 )
-            return xs_bank
+            xs_banks[j, i] = xs_bank
 
-        def second_matmul(j, i, xs_codes, xs_scales):
+        def second_matmul(j, i):
             h = j // CHUNKS_PER_HEAD
             tokens = slice(i * P, (i + 1) * P)
             out_bank = psum.tile([P, FEATURES], F32, tag="out_bank")
             nc.tensor.matmul_mx(
                 out=out_bank[:],
-                lhsT=xs_codes[:, tokens].bitcast(FP8X4),
-                lhsT_scale=xs_scales[:, tokens],
+                lhsT=xs_codes[j][:, tokens].bitcast(FP8X4),
+                lhsT_scale=xs_scales[j][:, tokens],
                 rhs=w_codes[h][:].bitcast(FP8X4),
                 rhs_scale=w_scales[h][:],
                 start=True,
                 stop=True,
             )
-            return out_bank
+            out_banks[j, i] = out_bank
 
-        def store_chunk(j, out_banks, copies):
+        xs_banks = {}
+        out_banks = {}
+        xs_grouped = {}
+        xs_codes = {}
+        xs_scales = {}
+
+        def start_chunk(j):
+            xs_grouped[j] = stage.tile([P, CHUNK, P, PACK], BF16, name="xs_grouped", align_bytes=64)
+            xs_codes[j] = stage.tile([P, CHUNK_TOKENS], U32, name="xs_codes", align_bytes=64)
+            xs_scales[j] = stage.tile([P, CHUNK_TOKENS], U8, name="xs_scales", align_bytes=64)
+
+        def copy_xs(j, i, copy):
+            copy(out=xs_grouped[j][:, i, :, :], in_=xs_banks[j, i][:].rearrange("p t c -> p c t"))
+
+        def quantise_xs(j, first, count):
+            tiles = slice(first, first + count)
+            tokens = slice(first * P, (first + count) * P)
+            nc.vector.quantize_mx(
+                out=xs_codes[j][:, tokens].bitcast(FP8X4),
+                scales=xs_scales[j][:, tokens],
+                in_=xs_grouped[j][:, tiles, :, :].rearrange("p i c t -> p (i c t)"),
+            )
+
+        def copy_out(j, i, copy):
             h = j // CHUNKS_PER_HEAD
             out_tiles = out[h].rearrange("(c r) e -> c r e", r=TOKEN_TILES)
-            for i in range(CHUNK):
-                out_rows = store.tile([P, FEATURES], F32)
-                copies[i % len(copies)](
-                    out=out_rows[:].rearrange("p (m t) -> p m t", t=PACK),
-                    in_=out_banks[i][:].rearrange("p (t m) -> p m t", t=PACK),
-                )
-                nc.sync.dma_start(out=out_tiles[:, (j % CHUNKS_PER_HEAD) * CHUNK + i, :], in_=out_rows[:])
+            out_rows = store.tile([P, FEATURES], F32)
+            copy(
+                out=out_rows[:].rearrange("p (m t) -> p m t", t=PACK),
+                in_=out_banks[j, i][:].rearrange("p (t m) -> p m t", t=PACK),
+            )
+            nc.sync.dma_start(out=out_tiles[:, (j % CHUNKS_PER_HEAD) * CHUNK + i, :], in_=out_rows[:])
 
-        for r in range(TOKEN_TILES):
-            transpose_x(r)
-        regroup_w(0, on_gpsimd=False)
-        regroup_w(1, on_gpsimd=False)
+        scalar = nc.scalar.copy
+        vector = nc.vector.tensor_copy
+
+        regroup_w(0, nc.vector)
+        regroup_w(1, nc.vector)
         quantise_w(0)
         quantise_w(1)
+        for r in range(CHUNK):
+            transpose_x(r)
         quantise_x(0)
-        regroup_w(2, on_gpsimd=False)
-        regroup_w(3, on_gpsimd=False)
-        quantise_w(2)
         quantise_x(1)
-        regroup_w(4, on_gpsimd=False)
-        xs_banks = [first_matmul(0, i) for i in range(CHUNK)]
-        out_banks = []
+        for i in range(CHUNK):
+            first_matmul(0, i)
+        nc.vector.memset(w_grouped[1][:, 0, :], 0.0)
+        regroup_w(3, nc.gpsimd)
+        regroup_w(2, nc.scalar)
+        start_chunk(0)
+        copy_xs(0, 0, scalar)
+        for r in range(CHUNK, TOKEN_TILES):
+            transpose_x(r)
+        for i in range(1, CHUNK):
+            copy_xs(0, i, vector)
+        quantise_w(2)
+        quantise_x(2)
+        quantise_x(3)
+        quantise_w(3)
+        quantise_xs(0, 0, CHUNK)
+        regroup_w(4, nc.gpsimd)
+        for i in range(CHUNK):
+            first_matmul(1, i)
+        for i in range(CHUNK):
+            second_matmul(0, i)
 
-        for j in range(CHUNKS):
-            xs_grouped = stage.tile([P, CHUNK, P, PACK], BF16, align_bytes=64)
-            xs_codes = stage.tile([P, CHUNK_TOKENS], U32, align_bytes=64)
-            xs_scales = stage.tile([P, CHUNK_TOKENS], U8, align_bytes=64)
-            next_xs_banks = []
-            scalar_xs_banks = SCALAR_XS_BANKS
-            if j == 0:
-                scalar_xs_banks = SCALAR_XS_BANKS_FIRST_ROUND
-            if j == CHUNKS - 1:
-                scalar_xs_banks = SCALAR_XS_BANKS_LAST_ROUND
+        for j in range(1, CHUNKS - 3):
+            start_chunk(j)
+            copy_xs(j, 0, scalar)
+            first_matmul(j + 1, 0)
             for i in range(CHUNK):
-                if i == scalar_xs_banks and j > 0:
-                    store_chunk(j - 1, out_banks, [nc.scalar.copy])
-                copy = nc.scalar.copy if i < scalar_xs_banks else nc.vector.tensor_copy
-                copy(out=xs_grouped[:, i, :, :], in_=xs_banks[i][:].rearrange("p t c -> p c t"))
-                if j + 1 < CHUNKS:
-                    next_xs_banks.append(first_matmul(j + 1, i))
+                copy_out(j - 1, i, scalar)
+            for i in range(1, CHUNK):
+                copy_xs(j, i, vector)
+                first_matmul(j + 1, i)
             if j + 3 < W_HALVES:
                 quantise_w(j + 3)
-            if j + 5 < W_HALVES:
-                regroup_w(j + 5, on_gpsimd=True)
-            nc.vector.quantize_mx(
-                out=xs_codes[:].bitcast(FP8X4),
-                scales=xs_scales[:],
-                in_=xs_grouped[:].rearrange("p i c t -> p (i c t)"),
-            )
-            out_banks = [second_matmul(j, i, xs_codes, xs_scales) for i in range(CHUNK)]
-            xs_banks = next_xs_banks
-        store_chunk(CHUNKS - 1, out_banks, [nc.scalar.copy, nc.vector.tensor_copy])
+            if j + 4 < W_HALVES:
+                regroup_w(j + 4, nc.gpsimd)
+            quantise_xs(j, 0, CHUNK)
+            for i in range(CHUNK):
+                second_matmul(j, i)
+
+        pairs = [(j, first) for j in range(CHUNKS - 3, CHUNKS) for first in (0, 2)]
+        tiles = [(j, i) for j in range(CHUNKS - 3, CHUNKS) for i in range(CHUNK)]
+        start_chunk(CHUNKS - 3)
+        copy_xs(CHUNKS - 3, 0, vector)
+        first_matmul(CHUNKS - 2, 0)
+        copied = 1
+        for n, (j, first) in enumerate(pairs):
+            for tile in tiles[copied : 2 * n + 3]:
+                if tile[1] == 0:
+                    start_chunk(tile[0])
+                copy_xs(tile[0], tile[1], vector)
+                if tile[0] + 1 < CHUNKS:
+                    first_matmul(tile[0] + 1, tile[1])
+            copied = 2 * n + 3
+            if n == 0:
+                for i in range(CHUNK):
+                    copy_out(j - 1, i, scalar)
+            else:
+                previous = pairs[n - 1]
+                copy_out(previous[0], previous[1], scalar)
+                if n + 1 < len(pairs):
+                    copy_out(previous[0], previous[1] + 1, scalar)
+            quantise_xs(j, first, 2)
+            second_matmul(j, first)
+            second_matmul(j, first + 1)
+        copy_out(CHUNKS - 1, 1, vector)
+        copy_out(CHUNKS - 1, 2, scalar)
+        copy_out(CHUNKS - 1, 3, vector)

@@ -34,7 +34,7 @@ def tile_multiheadattention_pa_kernel(tc, x, w, out):
     with ExitStack() as ctx:
         keep = ctx.enter_context(tc.tile_pool(name="keep", bufs=1))
         stage = ctx.enter_context(tc.tile_pool(name="stage", bufs=2))
-        store = ctx.enter_context(tc.tile_pool(name="store", bufs=12))
+        store = ctx.enter_context(tc.tile_pool(name="store", bufs=HEADS * TOKEN_TILES))
         psum = ctx.enter_context(tc.psum_pool(name="psum", bufs=CHUNK))
         ctx.enter_context(tc.manual_schedule())
 

@@ -72,7 +72,7 @@ def tile_multiheadattention_pa_kernel(tc, x, w, out):
         def regroup_w(m, engine):
             rows = w_rows[m // 2][:].rearrange("p t (c s) -> p c s t", s=PACK)
             rows = rows[:, :, (m % 2) * 2 : (m % 2) * 2 + 2, :]
-            grouped = w_grouped[0 if m in (0, 2) else 1][:].rearrange("p (s c) t -> p c s t", s=2)
+            grouped = w_grouped[m % 2][:].rearrange("p (s c) t -> p c s t", s=2)
             if engine is nc.gpsimd:
                 nc.gpsimd.tensor_scalar(
                     out=grouped,
@@ -92,7 +92,7 @@ def tile_multiheadattention_pa_kernel(tc, x, w, out):
             nc.vector.quantize_mx(
                 out=w_codes[m // 2][:, columns].bitcast(FP8X4),
                 scales=w_scales[m // 2][:, columns],
-                in_=w_grouped[0 if m in (0, 2) else 1][:].rearrange("p n t -> p (n t)"),
+                in_=w_grouped[m % 2][:].rearrange("p n t -> p (n t)"),
             )
 
         x_grouped = keep.tile([P, TOKEN_TILES, P * PACK], BF16, align_bytes=64)
@@ -210,36 +210,38 @@ def tile_multiheadattention_pa_kernel(tc, x, w, out):
         quantise_w(2)
         quantise_x(2)
         quantise_x(3)
+        regroup_w(4, nc.scalar)
         quantise_w(3)
+        regroup_w(5, nc.gpsimd)
         quantise_xs(0, 0, CHUNK)
-        regroup_w(4, nc.gpsimd)
         for i in range(CHUNK):
             first_matmul(1, i)
         for i in range(CHUNK):
             second_matmul(0, i)
+        start_chunk(1)
+        copy_xs(1, 0, scalar)
+        first_matmul(2, 0)
 
         for j in range(1, CHUNKS - 3):
-            start_chunk(j)
-            copy_xs(j, 0, scalar)
-            first_matmul(j + 1, 0)
-            for i in range(CHUNK):
+            start_chunk(j + 1)
+            for i in range(CHUNK - 1):
                 copy_out(j - 1, i, scalar)
             for i in range(1, CHUNK):
                 copy_xs(j, i, vector)
                 first_matmul(j + 1, i)
+            copy_xs(j + 1, 0, scalar)
+            copy_out(j - 1, CHUNK - 1, scalar)
             if j + 3 < W_HALVES:
                 quantise_w(j + 3)
-            if j + 4 < W_HALVES:
-                regroup_w(j + 4, nc.gpsimd)
+            if j + 5 < W_HALVES:
+                regroup_w(j + 5, nc.gpsimd)
             quantise_xs(j, 0, CHUNK)
             for i in range(CHUNK):
                 second_matmul(j, i)
+            first_matmul(j + 2, 0)
 
         pairs = [(j, first) for j in range(CHUNKS - 3, CHUNKS) for first in (0, 2)]
         tiles = [(j, i) for j in range(CHUNKS - 3, CHUNKS) for i in range(CHUNK)]
-        start_chunk(CHUNKS - 3)
-        copy_xs(CHUNKS - 3, 0, vector)
-        first_matmul(CHUNKS - 2, 0)
         copied = 1
         for n, (j, first) in enumerate(pairs):
             for tile in tiles[copied : 2 * n + 3]:

@@ -214,7 +214,7 @@ def tile_multiheadattention_pa_kernel(tc, x, w, out):
         quantise_w(3)
         regroup_w(5, nc.gpsimd)
         quantise_xs(0, 0, CHUNK)
-        for i in range(CHUNK):
+        for i in (0, 3, 2, 1):
             first_matmul(1, i)
         for i in range(CHUNK):
             second_matmul(0, i)
@@ -226,9 +226,9 @@ def tile_multiheadattention_pa_kernel(tc, x, w, out):
             start_chunk(j + 1)
             for i in range(CHUNK - 1):
                 copy_out(j - 1, i, scalar)
-            for i in range(1, CHUNK):
+            for n, i in enumerate(reversed(range(1, CHUNK))):
                 copy_xs(j, i, vector)
-                first_matmul(j + 1, i)
+                first_matmul(j + 1, n + 1 if j == CHUNKS - 4 else i)
             copy_xs(j + 1, 0, scalar)
             copy_out(j - 1, CHUNK - 1, scalar)
             if j + 3 < W_HALVES:

from contextlib import ExitStack

import concourse.mybir as mybir
from concourse.masks import make_identity

BF16 = mybir.dt.bfloat16
F32 = mybir.dt.float32
U32 = mybir.dt.uint32
U8 = mybir.dt.uint8
FP8X4 = mybir.dt.float8_e4m3fn_x4

P = 128
PACK = 4
HEADS = 8
TOKENS = 1024
FEATURES = P * PACK
TOKEN_TILES = TOKENS // P
CHUNK = 4
CHUNKS_PER_HEAD = TOKEN_TILES // CHUNK
CHUNKS = HEADS * CHUNKS_PER_HEAD
CHUNK_TOKENS = CHUNK * P
W_HALF = FEATURES // 2
W_HALVES = 2 * HEADS

WARM_UP_MATMULS = 5

FLOPS = 2 * 2 * HEADS * TOKENS * FEATURES * FEATURES


def tile_multiheadattention_pa_kernel(tc, x, w, out):
    nc = tc.nc
    x_tiles = x[0].rearrange("(c r) k -> c r k", r=TOKEN_TILES)

    with ExitStack() as ctx:
        keep = ctx.enter_context(tc.tile_pool(name="keep", bufs=1))
        stage = ctx.enter_context(tc.tile_pool(name="stage", bufs=2))
        store = ctx.enter_context(tc.tile_pool(name="store", bufs=HEADS * TOKEN_TILES))
        psum = ctx.enter_context(tc.psum_pool(name="psum", bufs=CHUNK))
        ctx.enter_context(tc.manual_schedule())

        x_rows = keep.tile([P, TOKEN_TILES, FEATURES], BF16)
        w_rows = [keep.tile([P, PACK, FEATURES], BF16, name="w_rows%d" % h) for h in range(HEADS)]

        def load_x(first, count):
            tiles = slice(first, first + count)
            nc.sync.dma_start(out=x_rows[:, tiles, :], in_=x_tiles[:, tiles, :])

        def load_w(h):
            nc.sync.dma_start(out=w_rows[h][:], in_=w[h].rearrange("(p t) n -> p t n", t=PACK))

        load_w(0)
        load_x(0, 2)
        load_x(2, 2)
        load_w(1)
        load_x(4, 4)
        for h in range(2, HEADS):
            load_w(h)

        identity = keep.tile([P, P], F32)
        make_identity(nc, identity[:])

        zeros = keep.tile([P, FEATURES], BF16)
        nc.vector.memset(zeros[:], 0.0)
        warm_bank = psum.tile([P, FEATURES], F32, tag="out_bank")
        for n in range(WARM_UP_MATMULS):
            nc.tensor.matmul(warm_bank[:], lhsT=zeros[:, :P], rhs=zeros[:], start=True, stop=True)

        w_codes = [keep.tile([P, FEATURES], U32, name="w_codes%d" % h, align_bytes=64) for h in range(HEADS)]
        w_scales = [keep.tile([P, FEATURES], U8, name="w_scales%d" % h, align_bytes=64) for h in range(HEADS)]
        w_grouped = [keep.tile([P, W_HALF, PACK], BF16, name="w_grouped%d" % s, align_bytes=64) for s in range(2)]

        def regroup_w(m, engine):
            rows = w_rows[m // 2][:].rearrange("p t (c s) -> p c s t", s=PACK)
            rows = rows[:, :, (m % 2) * 2 : (m % 2) * 2 + 2, :]
            grouped = w_grouped[m % 2][:].rearrange("p (s c) t -> p c s t", s=2)
            if engine is nc.gpsimd:
                nc.gpsimd.tensor_scalar(
                    out=grouped,
                    in0=rows,
                    scalar1=1.0,
                    scalar2=0.0,
                    op0=mybir.AluOpType.mult,
                    op1=mybir.AluOpType.add,
                )
            elif engine is nc.scalar:
                nc.scalar.copy(out=grouped, in_=rows)
            else:
                nc.vector.tensor_copy(out=grouped, in_=rows)

        def quantise_w(m):
            columns = slice((m % 2) * W_HALF, (m % 2 + 1) * W_HALF)
            nc.vector.quantize_mx(
                out=w_codes[m // 2][:, columns].bitcast(FP8X4),
                scales=w_scales[m // 2][:, columns],
                in_=w_grouped[m % 2][:].rearrange("p n t -> p (n t)"),
            )

        x_grouped = keep.tile([P, TOKEN_TILES, P * PACK], BF16, align_bytes=64)
        x_codes = keep.tile([P, TOKENS], U32, align_bytes=64)
        x_scales = keep.tile([P, TOKENS], U8, align_bytes=64)

        def transpose_x(r):
            x_bank = psum.tile([P, 2, P], F32, tag="xs_bank" if r < CHUNK else "out_bank")
            words = x_rows[:, r, :].bitcast(F32)
            for u in range(2):
                nc.tensor.transpose(x_bank[:, u, :], words[:, u : 2 * P : 2], identity[:])
            grouped_words = x_grouped[:, r, :].bitcast(F32)
            nc.scalar.copy(
                out=grouped_words.rearrange("p (c u) -> p c u", u=2),
                in_=x_bank[:].rearrange("p u c -> p c u"),
            )

        def quantise_x(pair):
            tiles = slice(pair * 2, (pair + 1) * 2)
            tokens = slice(pair * 2 * P, (pair + 1) * 2 * P)
            nc.vector.quantize_mx(
                out=x_codes[:, tokens].bitcast(FP8X4),
                scales=x_scales[:, tokens],
                in_=x_grouped[:, tiles, :].rearrange("p r k -> p (r k)"),
            )

        def first_matmul(j, i):
            h = j // CHUNKS_PER_HEAD
            r = (j % CHUNKS_PER_HEAD) * CHUNK + i
            tokens = slice(r * P, (r + 1) * P)
            xs_bank = psum.tile([P, PACK, P], F32, tag="xs_bank")
            for t in range(PACK):
                features = slice(t * P, (t + 1) * P)
                nc.tensor.matmul_mx(
                    out=xs_bank[:, t, :],
                    lhsT=w_codes[h][:, features].bitcast(FP8X4),
                    lhsT_scale=w_scales[h][:, features],
                    rhs=x_codes[:, tokens].bitcast(FP8X4),
                    rhs_scale=x_scales[:, tokens],
                    start=True,
                    stop=True,
                )
            xs_banks[j, i] = xs_bank

        def second_matmul(j, i):
            h = j // CHUNKS_PER_HEAD
            tokens = slice(i * P, (i + 1) * P)
            out_bank = psum.tile([P, FEATURES], F32, tag="out_bank")
            nc.tensor.matmul_mx(
                out=out_bank[:],
                lhsT=xs_codes[j][:, tokens].bitcast(FP8X4),
                lhsT_scale=xs_scales[j][:, tokens],
                rhs=w_codes[h][:].bitcast(FP8X4),
                rhs_scale=w_scales[h][:],
                start=True,
                stop=True,
            )
            out_banks[j, i] = out_bank

        xs_banks = {}
        out_banks = {}
        xs_grouped = {}
        xs_codes = {}
        xs_scales = {}

        def start_chunk(j):
            xs_grouped[j] = stage.tile([P, CHUNK, P, PACK], BF16, name="xs_grouped", align_bytes=64)
            xs_codes[j] = stage.tile([P, CHUNK_TOKENS], U32, name="xs_codes", align_bytes=64)
            xs_scales[j] = stage.tile([P, CHUNK_TOKENS], U8, name="xs_scales", align_bytes=64)

        def copy_xs(j, i, copy):
            copy(out=xs_grouped[j][:, i, :, :], in_=xs_banks[j, i][:].rearrange("p t c -> p c t"))

        def quantise_xs(j, first, count):
            tiles = slice(first, first + count)
            tokens = slice(first * P, (first + count) * P)
            nc.vector.quantize_mx(
                out=xs_codes[j][:, tokens].bitcast(FP8X4),
                scales=xs_scales[j][:, tokens],
                in_=xs_grouped[j][:, tiles, :, :].rearrange("p i c t -> p (i c t)"),
            )

        def copy_out(j, i, copy):
            h = j // CHUNKS_PER_HEAD
            out_tiles = out[h].rearrange("(c r) e -> c r e", r=TOKEN_TILES)
            out_rows = store.tile([P, FEATURES], F32)
            copy(
                out=out_rows[:].rearrange("p (m t) -> p m t", t=PACK),
                in_=out_banks[j, i][:].rearrange("p (t m) -> p m t", t=PACK),
            )
            nc.sync.dma_start(out=out_tiles[:, (j % CHUNKS_PER_HEAD) * CHUNK + i, :], in_=out_rows[:])

        scalar = nc.scalar.copy
        vector = nc.vector.tensor_copy

        regroup_w(0, nc.vector)
        regroup_w(1, nc.vector)
        quantise_w(0)
        quantise_w(1)
        for r in range(CHUNK):
            transpose_x(r)
        quantise_x(0)
        quantise_x(1)
        for i in range(CHUNK):
            first_matmul(0, i)
        nc.vector.memset(w_grouped[1][:, 0, :], 0.0)
        regroup_w(3, nc.gpsimd)
        regroup_w(2, nc.scalar)
        start_chunk(0)
        copy_xs(0, 0, scalar)
        for r in range(CHUNK, TOKEN_TILES):
            transpose_x(r)
        for i in range(1, CHUNK):
            copy_xs(0, i, vector)
        quantise_w(2)
        quantise_x(2)
        quantise_x(3)
        regroup_w(4, nc.scalar)
        quantise_w(3)
        regroup_w(5, nc.gpsimd)
        quantise_xs(0, 0, CHUNK)
        for i in (0, 3, 2, 1):
            first_matmul(1, i)
        for i in range(CHUNK):
            second_matmul(0, i)
        start_chunk(1)
        copy_xs(1, 0, scalar)
        first_matmul(2, 0)

        for j in range(1, CHUNKS - 3):
            start_chunk(j + 1)
            for i in range(CHUNK - 1):
                copy_out(j - 1, i, scalar)
            for n, i in enumerate(reversed(range(1, CHUNK))):
                copy_xs(j, i, vector)
                first_matmul(j + 1, n + 1 if j == CHUNKS - 4 else i)
            copy_xs(j + 1, 0, scalar)
            copy_out(j - 1, CHUNK - 1, scalar)
            if j + 3 < W_HALVES:
                quantise_w(j + 3)
            if j + 5 < W_HALVES:
                regroup_w(j + 5, nc.gpsimd)
            quantise_xs(j, 0, CHUNK)
            for i in range(CHUNK):
                second_matmul(j, i)
            first_matmul(j + 2, 0)

        pairs = [(j, first) for j in range(CHUNKS - 3, CHUNKS) for first in (0, 2)]
        tiles = [(j, i) for j in range(CHUNKS - 3, CHUNKS) for i in range(CHUNK)]
        copied = 1
        for n, (j, first) in enumerate(pairs):
            for tile in tiles[copied : 2 * n + 3]:
                if tile[1] == 0:
                    start_chunk(tile[0])
                copy_xs(tile[0], tile[1], vector)
                if tile[0] + 1 < CHUNKS:
                    first_matmul(tile[0] + 1, tile[1])
            copied = 2 * n + 3
            if n == 0:
                for i in range(CHUNK):
                    copy_out(j - 1, i, scalar)
            else:
                previous = pairs[n - 1]
                copy_out(previous[0], previous[1], scalar)
                if n + 1 < len(pairs):
                    copy_out(previous[0], previous[1] + 1, scalar)
            quantise_xs(j, first, 2)
            second_matmul(j, first)
            second_matmul(j, first + 1)
        copy_out(CHUNKS - 1, 1, vector)
        copy_out(CHUNKS - 1, 2, scalar)
        copy_out(CHUNKS - 1, 3, vector)
